import numpy as np
import ml_dtypes


def mxq(x, axis, fmt="e4m3"):
    dtype, down = {"e4m3": (ml_dtypes.float8_e4m3fn, 7), "e5m2": (ml_dtypes.float8_e5m2, 14)}[fmt]
    v = np.moveaxis(np.asarray(x, np.float32).astype(ml_dtypes.bfloat16).astype(np.float64), axis, -1)
    blocks = v.reshape(v.shape[:-1] + (-1, 32))
    amax = np.abs(blocks).max(-1, keepdims=True)
    byte = np.maximum(np.where(amax > 0, np.frexp(amax)[1] - 1 + 127, 0) - down, 1)
    scale = np.exp2(byte - 127.0)
    codes = (blocks / scale).astype(np.float32).astype(dtype).astype(np.float64)
    return np.moveaxis((codes * scale).reshape(v.shape), -1, axis)


WIDE = False


def mx_kscale(k):
    if not WIDE:
        return np.ones(k)
    levels = np.array([10, -10, 5, -5, 0])
    a = np.random.permutation(np.resize(levels, k // 512 * 4)).reshape(k // 512, 4)
    idx = np.arange(k)
    return np.exp2(a[idx // 512, idx % 128 // 32])


BF16 = ml_dtypes.bfloat16


def bf(x):
    return np.asarray(x, np.float32).astype(BF16)


def f64(x):
    return np.asarray(x).astype(np.float64)


E2M1 = np.array([0.0, 0.5, 1.0, 1.5, 2.0, 3.0, 4.0, 6.0, -0.0, -0.5, -1.0, -1.5, -2.0, -3.0, -4.0, -6.0])


def pack_weight(w, fmt):
    k, n = w.shape
    w = f64(bf(w)).reshape(k // 32, 32, n)
    amax = np.abs(w).max(1)
    if fmt == "e4m3":
        byte = np.frexp(amax)[1] - 1 + 127 - 7
    else:
        mant, ex = np.frexp(amax / 6.0)
        byte = np.where(mant > 0.5, ex, ex - 1) + 127
    byte = np.clip(np.where(amax > 0, byte, 1), 1, 254)
    scaled = (w * np.exp2(127.0 - byte)[:, None, :]).reshape(k, n).astype(np.float32)
    by_word = np.ascontiguousarray(scaled.reshape(k // 512, 128, 4, n).transpose(0, 1, 3, 2))
    if fmt == "e4m3":
        words = by_word.astype(ml_dtypes.float8_e4m3fn).view(np.uint8)
    else:
        c = by_word.astype(ml_dtypes.float4_e2m1fn).view(np.uint8) & 0xF
        words = c[..., 0::2] | (c[..., 1::2] << 4)
    return np.ascontiguousarray(words), np.ascontiguousarray(byte.astype(np.uint8).reshape(k // 512, 16, n))


def unpack_weight(words, scales, fmt):
    g, p, n, _ = words.shape
    if fmt == "e4m3":
        vals = np.ascontiguousarray(words).view(ml_dtypes.float8_e4m3fn).astype(np.float64)
    else:
        nib = np.empty((g, p, n, 4), np.uint8)
        nib[..., 0::2] = words & 0xF
        nib[..., 1::2] = words >> 4
        vals = E2M1[nib]
    vals = vals * np.repeat(np.exp2(scales.astype(np.float64) - 127.0), 8, axis=1)[..., None]
    return vals.transpose(0, 1, 3, 2).reshape(g * 512, n)

def pack4(w):
    words, scales = pack_weight(w, "e2m1")
    return words.reshape(words.shape[0], 128, -1), scales


def unpack4(words, scales):
    return unpack_weight(words.reshape(words.shape[0], 128, -1, 2), scales, "e2m1")


B, S, K, N = 2, 512, 2048, 2048


def setup_inputs():
    s = mx_kscale(K)
    input = bf(np.random.standard_normal((B, S, K)) * s)
    weight = np.random.standard_normal((N, K)) / np.sqrt(K) / s[None, :]
    words, scales = pack4(np.ascontiguousarray(weight.T))
    bias = bf(np.random.standard_normal(N) * 0.5)
    return {"input": input,
            "weight_words": words,
            "weight_scales": scales,
            "bias": bias}


def reference(input, weight_words, weight_scales, bias):
    xq = mxq(f64(input), 2, "e4m3")
    wq = unpack4(weight_words, weight_scales)
    out = xq.reshape(B * S, K) @ wq
    return out.reshape(B, S, N) + f64(bias)

@@ -1,0 +1,183 @@
+from contextlib import ExitStack
+
+import concourse.mybir as mybir
+from concourse.masks import make_identity
+
+F32 = mybir.dt.float32
+BF16 = mybir.dt.bfloat16
+I32 = mybir.dt.int32
+U32 = mybir.dt.uint32
+U8 = mybir.dt.uint8
+FP8X4 = mybir.dt.float8_e4m3fn_x4
+FP4X4 = mybir.dt.float4_e2m1fn_x4
+ADD = mybir.AluOpType.add
+
+P = 128
+TOKENS = 1024
+K = 2048
+N = 2048
+K_PASS = 512
+PASSES = K // K_PASS
+N_CHUNK = 512
+CHUNKS = N // N_CHUNK
+ROW_TILES = TOKENS // P
+
+FLOPS = 2 * TOKENS * K * N
+
+
+def tile_tiledlinear_kernel(tc, x, weight_words, weight_scales, bias, out):
+    nc = tc.nc
+    x_rows = x.flatten_outer_dims()
+    out_rows = out.flatten_outer_dims()
+
+    with ExitStack() as ctx:
+        ctx.enter_context(tc.manual_schedule())
+        keep = ctx.enter_context(tc.tile_pool(name="keep", bufs=1))
+        ring = ctx.enter_context(tc.tile_pool(name="ring", bufs=4))
+        acc_pool = ctx.enter_context(tc.psum_pool(name="acc_pool", bufs=4))
+        tp_pool = ctx.enter_context(tc.psum_pool(name="tp_pool", bufs=4))
+
+        x_sb = [keep.tile([P, K], BF16, name="x_sb%d" % i) for i in range(ROW_TILES)]
+        w_sb = [keep.tile([P, PASSES, 2 * N_CHUNK], U8, name="w_sb%d" % c, align_bytes=64) for c in range(CHUNKS)]
+        w_sc = [keep.tile([P, PASSES, N_CHUNK], U8, name="w_sc%d" % c, align_bytes=64) for c in range(CHUNKS)]
+        x_q = [keep.tile([P, PASSES * P], U32, name="x_q%d" % i, align_bytes=64) for i in range(ROW_TILES)]
+        x_qs = [keep.tile([P, PASSES * P], U8, name="x_qs%d" % i, align_bytes=64) for i in range(ROW_TILES)]
+        bias_f = [keep.tile([P, N_CHUNK], F32, name="bias_f%d" % c) for c in range(CHUNKS)]
+        bias_row = keep.tile([P, N], BF16, name="bias_row")
+        ones = keep.tile([P, P], BF16, name="ones")
+        ident = keep.tile([P, P], F32, name="ident")
+
+        nc.vector.memset(bias_row[:], 0.0)
+        nc.vector.memset(ones[:], 1.0)
+        for c in range(CHUNKS):
+            nc.vector.memset(w_sc[c][:].bitcast(I32), 0)
+        make_identity(nc, ident[:])
+
+        nc.scalar.dma_start(out=bias_row[0:1, :], in_=bias.rearrange("(o n) -> o n", o=1))
+
+        def load_x(i, pieces):
+            width = K // pieces
+            for h in range(pieces):
+                cols = slice(h * width, (h + 1) * width)
+                nc.sync.dma_start(out=x_sb[i][:, cols], in_=x_rows[i * P : (i + 1) * P, cols])
+
+        def load_scales(c):
+            src = weight_scales[:, :, c * N_CHUNK : (c + 1) * N_CHUNK].bitcast(I32).rearrange("g q b -> q g b")
+            for r in range(4):
+                nc.sync.dma_start(out=w_sc[c][r:P:32].bitcast(I32), in_=src[r:16:4])
+
+        def load_words(c):
+            src = weight_words[:, :, c * 2 * N_CHUNK : (c + 1) * 2 * N_CHUNK].bitcast(I32).rearrange("g p b -> p g b")
+            nc.sync.dma_start(out=w_sb[c][:].bitcast(I32), in_=src)
+
+        load_x(0, 2)
+        load_x(1, 1)
+        load_scales(0)
+        load_words(0)
+        load_scales(1)
+        load_words(1)
+        load_x(2, 1)
+        load_x(3, 1)
+        load_scales(2)
+        load_words(2)
+        load_scales(3)
+        load_words(3)
+        for i in range(4, ROW_TILES):
+            load_x(i, 1)
+
+        for c in range(CHUNKS):
+            acc = acc_pool.tile([P, N_CHUNK], F32, name="acc", tag="acc")
+            nc.tensor.matmul(out=acc[:], lhsT=ones[:], rhs=bias_row[:, c * N_CHUNK : (c + 1) * N_CHUNK], start=True, stop=True)
+            if c % 2 == 0:
+                nc.vector.tensor_copy(out=bias_f[c][:], in_=acc[:])
+            else:
+                nc.scalar.copy(out=bias_f[c][:], in_=acc[:])
+
+        sorted_words = {}
+        grouped = {}
+
+        def sort_words(i):
+            t = ring.tile([P, 2, K // 4], F32, name="sorted_w", tag="sorted_w")
+            nc.scalar.copy(out=t[:], in_=x_sb[i][:].bitcast(F32).rearrange("r (q u) -> r u q", u=2))
+            sorted_words[i] = t
+
+        def transposes(i, vector_helps):
+            grp = ring.tile([P, K], BF16, name="grouped", tag="grouped", align_bytes=64)
+            grouped[i] = grp
+            x32 = x_sb[i][:].bitcast(F32)
+            for b in range(2):
+                tp = tp_pool.tile([P, 2, 2, P], F32, name="tp", tag="tp")
+                for gl in range(2):
+                    g = 2 * b + gl
+                    for u in range(2):
+                        if i in sorted_words:
+                            src = sorted_words[i][:, u, g * P : (g + 1) * P]
+                        else:
+                            src = x32[:, 256 * g + u : 256 * (g + 1) : 2]
+                        nc.tensor.transpose(tp[:, gl, u, :], src, ident[:])
+                dst = grp[:].bitcast(F32)[:, 512 * b : 512 * (b + 1)].rearrange("p (g r u) -> p g r u", g=2, u=2)
+                if vector_helps and b == 1:
+                    nc.vector.tensor_copy(out=dst, in_=tp[:].rearrange("p g u r -> p g r u"))
+                else:
+                    nc.scalar.copy(out=dst, in_=tp[:].rearrange("p g u r -> p g r u"))
+
+        def quantise(i):
+            for b in range(2):
+                nc.vector.quantize_mx(
+                    out=x_q[i][:, 256 * b : 256 * (b + 1)].bitcast(FP8X4),
+                    scales=x_qs[i][:, 256 * b : 256 * (b + 1)],
+                    in_=grouped[i][:, 1024 * b : 1024 * (b + 1)],
+                )
+
+        def block(i, c):
+            acc = acc_pool.tile([P, N_CHUNK], F32, name="acc", tag="acc")
+            for g in range(PASSES):
+                nc.tensor.matmul_mx(
+                    out=acc[:],
+                    lhsT=x_q[i][:, g * P : (g + 1) * P].bitcast(FP8X4),
+                    lhsT_scale=x_qs[i][:, g * P : (g + 1) * P],
+                    rhs=w_sb[c][:, g, :].bitcast(FP4X4),
+                    rhs_scale=w_sc[c][:, g, :],
+                    start=(g == 0),
+                    stop=(g == PASSES - 1),
+                )
+            res = keep.tile([P, N_CHUNK], F32, name="res%d_%d" % (i, c))
+            nc.vector.tensor_tensor(out=res[:], in0=acc[:], in1=bias_f[c][:], op=ADD)
+            nc.sync.dma_start(out=out_rows[i * P : (i + 1) * P, c * N_CHUNK : (c + 1) * N_CHUNK], in_=res[:])
+
+        transposes(0, True)
+        quantise(0)
+        transposes(1, True)
+        quantise(1)
+        sort_words(2)
+        sort_words(3)
+        for i, c in ((0, 0), (1, 0), (0, 1), (1, 1)):
+            block(i, c)
+        transposes(2, False)
+        transposes(3, False)
+        sort_words(4)
+        sort_words(5)
+        quantise(2)
+        block(0, 2)
+        quantise(3)
+        for i, c in ((1, 2), (2, 0), (2, 1), (2, 2), (0, 3), (1, 3), (2, 3)):
+            block(i, c)
+        transposes(4, False)
+        transposes(5, False)
+        sort_words(6)
+        sort_words(7)
+        quantise(4)
+        block(3, 0)
+        quantise(5)
+        for i, c in ((3, 1), (3, 2), (3, 3), (4, 0), (4, 1), (4, 2), (4, 3)):
+            block(i, c)
+        transposes(6, False)
+        transposes(7, False)
+        quantise(6)
+        block(5, 0)
+        quantise(7)
+        for c in range(1, CHUNKS):
+            block(5, c)
+        for i in (6, 7):
+            for c in range(CHUNKS):
+                block(i, c)

@@ -53,7 +53,7 @@ def tile_tiledlinear_kernel(tc, x, weight_words, weight_scales, bias, out):
             nc.vector.memset(w_sc[c][:].bitcast(I32), 0)
         make_identity(nc, ident[:])
 
-        nc.scalar.dma_start(out=bias_row[0:1, :], in_=bias.rearrange("(o n) -> o n", o=1))
+        nc.sync.dma_start(out=bias_row[0:1, :], in_=bias.rearrange("(o n) -> o n", o=1))
 
         def load_x(i, pieces):
             width = K // pieces
@@ -88,35 +88,33 @@ def tile_tiledlinear_kernel(tc, x, weight_words, weight_scales, bias, out):
         for c in range(CHUNKS):
             acc = acc_pool.tile([P, N_CHUNK], F32, name="acc", tag="acc")
             nc.tensor.matmul(out=acc[:], lhsT=ones[:], rhs=bias_row[:, c * N_CHUNK : (c + 1) * N_CHUNK], start=True, stop=True)
-            if c % 2 == 0:
-                nc.vector.tensor_copy(out=bias_f[c][:], in_=acc[:])
-            else:
-                nc.scalar.copy(out=bias_f[c][:], in_=acc[:])
+            nc.vector.tensor_copy(out=bias_f[c][:], in_=acc[:])
 
         sorted_words = {}
         grouped = {}
 
-        def sort_words(i):
+        def sort_words(i, pieces):
             t = ring.tile([P, 2, K // 4], F32, name="sorted_w", tag="sorted_w")
-            nc.scalar.copy(out=t[:], in_=x_sb[i][:].bitcast(F32).rearrange("r (q u) -> r u q", u=2))
+            quads = K // 4 // pieces
+            x32 = x_sb[i][:].bitcast(F32)
+            for h in range(pieces):
+                nc.scalar.copy(
+                    out=t[:, :, h * quads : (h + 1) * quads],
+                    in_=x32[:, 2 * h * quads : 2 * (h + 1) * quads].rearrange("r (q u) -> r u q", u=2),
+                )
             sorted_words[i] = t
 
-        def transposes(i, vector_helps):
+        def transposes(i, copiers):
             grp = ring.tile([P, K], BF16, name="grouped", tag="grouped", align_bytes=64)
             grouped[i] = grp
-            x32 = x_sb[i][:].bitcast(F32)
             for b in range(2):
                 tp = tp_pool.tile([P, 2, 2, P], F32, name="tp", tag="tp")
                 for gl in range(2):
                     g = 2 * b + gl
                     for u in range(2):
-                        if i in sorted_words:
-                            src = sorted_words[i][:, u, g * P : (g + 1) * P]
-                        else:
-                            src = x32[:, 256 * g + u : 256 * (g + 1) : 2]
-                        nc.tensor.transpose(tp[:, gl, u, :], src, ident[:])
+                        nc.tensor.transpose(tp[:, gl, u, :], sorted_words[i][:, u, g * P : (g + 1) * P], ident[:])
                 dst = grp[:].bitcast(F32)[:, 512 * b : 512 * (b + 1)].rearrange("p (g r u) -> p g r u", g=2, u=2)
-                if vector_helps and b == 1:
+                if copiers[b] == "v":
                     nc.vector.tensor_copy(out=dst, in_=tp[:].rearrange("p g u r -> p g r u"))
                 else:
                     nc.scalar.copy(out=dst, in_=tp[:].rearrange("p g u r -> p g r u"))
@@ -145,34 +143,36 @@ def tile_tiledlinear_kernel(tc, x, weight_words, weight_scales, bias, out):
             nc.vector.tensor_tensor(out=res[:], in0=acc[:], in1=bias_f[c][:], op=ADD)
             nc.sync.dma_start(out=out_rows[i * P : (i + 1) * P, c * N_CHUNK : (c + 1) * N_CHUNK], in_=res[:])
 
-        transposes(0, True)
+        sort_words(0, 2)
+        sort_words(1, 1)
+        transposes(0, "vs")
         quantise(0)
-        transposes(1, True)
+        transposes(1, "sv")
         quantise(1)
-        sort_words(2)
-        sort_words(3)
+        sort_words(2, 1)
+        sort_words(3, 1)
         for i, c in ((0, 0), (1, 0), (0, 1), (1, 1)):
             block(i, c)
-        transposes(2, False)
-        transposes(3, False)
-        sort_words(4)
-        sort_words(5)
+        transposes(2, "ss")
+        transposes(3, "ss")
+        sort_words(4, 1)
+        sort_words(5, 1)
         quantise(2)
         block(0, 2)
         quantise(3)
         for i, c in ((1, 2), (2, 0), (2, 1), (2, 2), (0, 3), (1, 3), (2, 3)):
             block(i, c)
-        transposes(4, False)
-        transposes(5, False)
-        sort_words(6)
-        sort_words(7)
+        transposes(4, "ss")
+        transposes(5, "ss")
+        sort_words(6, 1)
+        sort_words(7, 1)
         quantise(4)
         block(3, 0)
         quantise(5)
         for i, c in ((3, 1), (3, 2), (3, 3), (4, 0), (4, 1), (4, 2), (4, 3)):
             block(i, c)
-        transposes(6, False)
-        transposes(7, False)
+        transposes(6, "ss")
+        transposes(7, "ss")
         quantise(6)
         block(5, 0)
         quantise(7)

@@ -47,13 +47,11 @@ def tile_tiledlinear_kernel(tc, x, weight_words, weight_scales, bias, out):
         ones = keep.tile([P, P], BF16, name="ones")
         ident = keep.tile([P, P], F32, name="ident")
 
-        nc.vector.memset(bias_row[:], 0.0)
+        nc.vector.memset(bias_row[:].bitcast(I32), 0)
         nc.vector.memset(ones[:], 1.0)
         for c in range(CHUNKS):
             nc.vector.memset(w_sc[c][:].bitcast(I32), 0)
         make_identity(nc, ident[:])
-
-        nc.sync.dma_start(out=bias_row[0:1, :], in_=bias.rearrange("(o n) -> o n", o=1))
 
         def load_x(i, pieces):
             width = K // pieces
@@ -71,6 +69,7 @@ def tile_tiledlinear_kernel(tc, x, weight_words, weight_scales, bias, out):
             nc.sync.dma_start(out=w_sb[c][:].bitcast(I32), in_=src)
 
         load_x(0, 2)
+        nc.sync.dma_start(out=bias_row[0:1, :], in_=bias.rearrange("(o n) -> o n", o=1))
         load_x(1, 1)
         load_scales(0)
         load_words(0)
@@ -85,39 +84,36 @@ def tile_tiledlinear_kernel(tc, x, weight_words, weight_scales, bias, out):
         for i in range(4, ROW_TILES):
             load_x(i, 1)
 
-        for c in range(CHUNKS):
-            acc = acc_pool.tile([P, N_CHUNK], F32, name="acc", tag="acc")
-            nc.tensor.matmul(out=acc[:], lhsT=ones[:], rhs=bias_row[:, c * N_CHUNK : (c + 1) * N_CHUNK], start=True, stop=True)
-            nc.vector.tensor_copy(out=bias_f[c][:], in_=acc[:])
+        def spread_bias():
+            for c in range(CHUNKS):
+                acc = acc_pool.tile([P, N_CHUNK], F32, name="acc", tag="acc")
+                nc.tensor.matmul(out=acc[:], lhsT=ones[:], rhs=bias_row[:, c * N_CHUNK : (c + 1) * N_CHUNK], start=True, stop=True)
+                nc.vector.tensor_copy(out=bias_f[c][:], in_=acc[:])
 
         sorted_words = {}
         grouped = {}
 
-        def sort_words(i, pieces):
+        def sort_words(i):
             t = ring.tile([P, 2, K // 4], F32, name="sorted_w", tag="sorted_w")
-            quads = K // 4 // pieces
-            x32 = x_sb[i][:].bitcast(F32)
-            for h in range(pieces):
-                nc.scalar.copy(
-                    out=t[:, :, h * quads : (h + 1) * quads],
-                    in_=x32[:, 2 * h * quads : 2 * (h + 1) * quads].rearrange("r (q u) -> r u q", u=2),
-                )
+            nc.scalar.copy(out=t[:], in_=x_sb[i][:].bitcast(F32).rearrange("r (q u) -> r u q", u=2))
             sorted_words[i] = t
 
-        def transposes(i, copiers):
+        def transposes(i):
             grp = ring.tile([P, K], BF16, name="grouped", tag="grouped", align_bytes=64)
             grouped[i] = grp
+            x32 = x_sb[i][:].bitcast(F32)
             for b in range(2):
                 tp = tp_pool.tile([P, 2, 2, P], F32, name="tp", tag="tp")
                 for gl in range(2):
                     g = 2 * b + gl
                     for u in range(2):
-                        nc.tensor.transpose(tp[:, gl, u, :], sorted_words[i][:, u, g * P : (g + 1) * P], ident[:])
+                        if i in sorted_words:
+                            src = sorted_words[i][:, u, g * P : (g + 1) * P]
+                        else:
+                            src = x32[:, 256 * g + u : 256 * (g + 1) : 2]
+                        nc.tensor.transpose(tp[:, gl, u, :], src, ident[:])
                 dst = grp[:].bitcast(F32)[:, 512 * b : 512 * (b + 1)].rearrange("p (g r u) -> p g r u", g=2, u=2)
-                if copiers[b] == "v":
-                    nc.vector.tensor_copy(out=dst, in_=tp[:].rearrange("p g u r -> p g r u"))
-                else:
-                    nc.scalar.copy(out=dst, in_=tp[:].rearrange("p g u r -> p g r u"))
+                nc.scalar.copy(out=dst, in_=tp[:].rearrange("p g u r -> p g r u"))
 
         def quantise(i):
             for b in range(2):
@@ -143,41 +139,30 @@ def tile_tiledlinear_kernel(tc, x, weight_words, weight_scales, bias, out):
             nc.vector.tensor_tensor(out=res[:], in0=acc[:], in1=bias_f[c][:], op=ADD)
             nc.sync.dma_start(out=out_rows[i * P : (i + 1) * P, c * N_CHUNK : (c + 1) * N_CHUNK], in_=res[:])
 
-        sort_words(0, 2)
-        sort_words(1, 1)
-        transposes(0, "vs")
+        transposes(0)
         quantise(0)
-        transposes(1, "sv")
+        spread_bias()
+        sort_words(1)
+        transposes(1)
         quantise(1)
-        sort_words(2, 1)
-        sort_words(3, 1)
-        for i, c in ((0, 0), (1, 0), (0, 1), (1, 1)):
-            block(i, c)
-        transposes(2, "ss")
-        transposes(3, "ss")
-        sort_words(4, 1)
-        sort_words(5, 1)
+        sort_words(2)
+        sort_words(3)
+        for i in (0, 1):
+            for c in (0, 1):
+                block(i, c)
+        transposes(2)
+        transposes(3)
         quantise(2)
-        block(0, 2)
         quantise(3)
-        for i, c in ((1, 2), (2, 0), (2, 1), (2, 2), (0, 3), (1, 3), (2, 3)):
-            block(i, c)
-        transposes(4, "ss")
-        transposes(5, "ss")
-        sort_words(6, 1)
-        sort_words(7, 1)
-        quantise(4)
-        block(3, 0)
-        quantise(5)
-        for i, c in ((3, 1), (3, 2), (3, 3), (4, 0), (4, 1), (4, 2), (4, 3)):
-            block(i, c)
-        transposes(6, "ss")
-        transposes(7, "ss")
-        quantise(6)
-        block(5, 0)
-        quantise(7)
-        for c in range(1, CHUNKS):
-            block(5, c)
-        for i in (6, 7):
+        for c in (2, 3):
+            for i in (0, 1):
+                block(i, c)
+        for i in range(2, ROW_TILES):
+            if i % 2 == 1 and i + 2 < ROW_TILES:
+                for j in (i + 1, i + 2):
+                    sort_words(j)
+                for j in (i + 1, i + 2):
+                    transposes(j)
+                    quantise(j)
             for c in range(CHUNKS):
                 block(i, c)

@@ -123,21 +123,23 @@ def tile_tiledlinear_kernel(tc, x, weight_words, weight_scales, bias, out):
                     in_=grouped[i][:, 1024 * b : 1024 * (b + 1)],
                 )
 
-        def block(i, c):
-            acc = acc_pool.tile([P, N_CHUNK], F32, name="acc", tag="acc")
-            for g in range(PASSES):
-                nc.tensor.matmul_mx(
-                    out=acc[:],
-                    lhsT=x_q[i][:, g * P : (g + 1) * P].bitcast(FP8X4),
-                    lhsT_scale=x_qs[i][:, g * P : (g + 1) * P],
-                    rhs=w_sb[c][:, g, :].bitcast(FP4X4),
-                    rhs_scale=w_sc[c][:, g, :],
-                    start=(g == 0),
-                    stop=(g == PASSES - 1),
-                )
-            res = keep.tile([P, N_CHUNK], F32, name="res%d_%d" % (i, c))
-            nc.vector.tensor_tensor(out=res[:], in0=acc[:], in1=bias_f[c][:], op=ADD)
-            nc.sync.dma_start(out=out_rows[i * P : (i + 1) * P, c * N_CHUNK : (c + 1) * N_CHUNK], in_=res[:])
+        def block(i, c, width):
+            for s in range(N_CHUNK // width):
+                acc = acc_pool.tile([P, N_CHUNK], F32, name="acc", tag="acc")
+                for g in range(PASSES):
+                    nc.tensor.matmul_mx(
+                        out=acc[:, 0:width],
+                        lhsT=x_q[i][:, g * P : (g + 1) * P].bitcast(FP8X4),
+                        lhsT_scale=x_qs[i][:, g * P : (g + 1) * P],
+                        rhs=w_sb[c][:, g, 2 * s * width : 2 * (s + 1) * width].bitcast(FP4X4),
+                        rhs_scale=w_sc[c][:, g, s * width : (s + 1) * width],
+                        start=(g == 0),
+                        stop=(g == PASSES - 1),
+                    )
+                res = keep.tile([P, width], F32, name="res%d_%d_%d" % (i, c, s))
+                nc.vector.tensor_tensor(out=res[:], in0=acc[:, 0:width], in1=bias_f[c][:, s * width : (s + 1) * width], op=ADD)
+                first = c * N_CHUNK + s * width
+                nc.sync.dma_start(out=out_rows[i * P : (i + 1) * P, first : first + width], in_=res[:])
 
         transposes(0)
         quantise(0)
@@ -149,14 +151,14 @@ def tile_tiledlinear_kernel(tc, x, weight_words, weight_scales, bias, out):
         sort_words(3)
         for i in (0, 1):
             for c in (0, 1):
-                block(i, c)
+                block(i, c, N_CHUNK)
         transposes(2)
         transposes(3)
         quantise(2)
         quantise(3)
         for c in (2, 3):
             for i in (0, 1):
-                block(i, c)
+                block(i, c, N_CHUNK)
         for i in range(2, ROW_TILES):
             if i % 2 == 1 and i + 2 < ROW_TILES:
                 for j in (i + 1, i + 2):
@@ -165,4 +167,5 @@ def tile_tiledlinear_kernel(tc, x, weight_words, weight_scales, bias, out):
                     transposes(j)
                     quantise(j)
             for c in range(CHUNKS):
-                block(i, c)
+                last = i == ROW_TILES - 1 and c == CHUNKS - 1
+                block(i, c, P if last else N_CHUNK)

@@ -39,7 +39,7 @@ def tile_tiledlinear_kernel(tc, x, weight_words, weight_scales, bias, out):
 
         x_sb = [keep.tile([P, K], BF16, name="x_sb%d" % i) for i in range(ROW_TILES)]
         w_sb = [keep.tile([P, PASSES, 2 * N_CHUNK], U8, name="w_sb%d" % c, align_bytes=64) for c in range(CHUNKS)]
-        w_sc = [keep.tile([P, PASSES, N_CHUNK], U8, name="w_sc%d" % c, align_bytes=64) for c in range(CHUNKS)]
+        w_sc = [keep.tile([P, PASSES, 2 * N_CHUNK], U8, name="w_sc%d" % h, align_bytes=64) for h in range(CHUNKS // 2)]
         x_q = [keep.tile([P, PASSES * P], U32, name="x_q%d" % i, align_bytes=64) for i in range(ROW_TILES)]
         x_qs = [keep.tile([P, PASSES * P], U8, name="x_qs%d" % i, align_bytes=64) for i in range(ROW_TILES)]
         bias_f = [keep.tile([P, N_CHUNK], F32, name="bias_f%d" % c) for c in range(CHUNKS)]
@@ -47,10 +47,10 @@ def tile_tiledlinear_kernel(tc, x, weight_words, weight_scales, bias, out):
         ones = keep.tile([P, P], BF16, name="ones")
         ident = keep.tile([P, P], F32, name="ident")
 
+        nc.vector.memset(w_sc[0][:].bitcast(I32), 0)
         nc.vector.memset(bias_row[:].bitcast(I32), 0)
         nc.vector.memset(ones[:], 1.0)
-        for c in range(CHUNKS):
-            nc.vector.memset(w_sc[c][:].bitcast(I32), 0)
+        nc.vector.memset(w_sc[1][:].bitcast(I32), 0)
         make_identity(nc, ident[:])
 
         def load_x(i, pieces):
@@ -59,10 +59,10 @@ def tile_tiledlinear_kernel(tc, x, weight_words, weight_scales, bias, out):
                 cols = slice(h * width, (h + 1) * width)
                 nc.sync.dma_start(out=x_sb[i][:, cols], in_=x_rows[i * P : (i + 1) * P, cols])
 
-        def load_scales(c):
-            src = weight_scales[:, :, c * N_CHUNK : (c + 1) * N_CHUNK].bitcast(I32).rearrange("g q b -> q g b")
+        for h in range(CHUNKS // 2):
+            src = weight_scales[:, :, 2 * h * N_CHUNK : 2 * (h + 1) * N_CHUNK].bitcast(F32).rearrange("g q b -> q g b")
             for r in range(4):
-                nc.sync.dma_start(out=w_sc[c][r:P:32].bitcast(I32), in_=src[r:16:4])
+                nc.gpsimd.dma_start(out=w_sc[h][r:P:32].bitcast(F32), in_=src[r:16:4])
 
         def load_words(c):
             src = weight_words[:, :, c * 2 * N_CHUNK : (c + 1) * 2 * N_CHUNK].bitcast(I32).rearrange("g p b -> p g b")
@@ -71,15 +71,11 @@ def tile_tiledlinear_kernel(tc, x, weight_words, weight_scales, bias, out):
         load_x(0, 2)
         nc.sync.dma_start(out=bias_row[0:1, :], in_=bias.rearrange("(o n) -> o n", o=1))
         load_x(1, 1)
-        load_scales(0)
         load_words(0)
-        load_scales(1)
         load_words(1)
         load_x(2, 1)
         load_x(3, 1)
-        load_scales(2)
         load_words(2)
-        load_scales(3)
         load_words(3)
         for i in range(4, ROW_TILES):
             load_x(i, 1)
@@ -123,23 +119,21 @@ def tile_tiledlinear_kernel(tc, x, weight_words, weight_scales, bias, out):
                     in_=grouped[i][:, 1024 * b : 1024 * (b + 1)],
                 )
 
-        def block(i, c, width):
-            for s in range(N_CHUNK // width):
-                acc = acc_pool.tile([P, N_CHUNK], F32, name="acc", tag="acc")
-                for g in range(PASSES):
-                    nc.tensor.matmul_mx(
-                        out=acc[:, 0:width],
-                        lhsT=x_q[i][:, g * P : (g + 1) * P].bitcast(FP8X4),
-                        lhsT_scale=x_qs[i][:, g * P : (g + 1) * P],
-                        rhs=w_sb[c][:, g, 2 * s * width : 2 * (s + 1) * width].bitcast(FP4X4),
-                        rhs_scale=w_sc[c][:, g, s * width : (s + 1) * width],
-                        start=(g == 0),
-                        stop=(g == PASSES - 1),
-                    )
-                res = keep.tile([P, width], F32, name="res%d_%d_%d" % (i, c, s))
-                nc.vector.tensor_tensor(out=res[:], in0=acc[:, 0:width], in1=bias_f[c][:, s * width : (s + 1) * width], op=ADD)
-                first = c * N_CHUNK + s * width
-                nc.sync.dma_start(out=out_rows[i * P : (i + 1) * P, first : first + width], in_=res[:])
+        def block(i, c):
+            acc = acc_pool.tile([P, N_CHUNK], F32, name="acc", tag="acc")
+            for g in range(PASSES):
+                nc.tensor.matmul_mx(
+                    out=acc[:],
+                    lhsT=x_q[i][:, g * P : (g + 1) * P].bitcast(FP8X4),
+                    lhsT_scale=x_qs[i][:, g * P : (g + 1) * P],
+                    rhs=w_sb[c][:, g, :].bitcast(FP4X4),
+                    rhs_scale=w_sc[c // 2][:, g, (c % 2) * N_CHUNK : (c % 2 + 1) * N_CHUNK],
+                    start=(g == 0),
+                    stop=(g == PASSES - 1),
+                )
+            res = keep.tile([P, N_CHUNK], F32, name="res%d_%d" % (i, c))
+            nc.vector.tensor_tensor(out=res[:], in0=acc[:], in1=bias_f[c][:], op=ADD)
+            nc.sync.dma_start(out=out_rows[i * P : (i + 1) * P, c * N_CHUNK : (c + 1) * N_CHUNK], in_=res[:])
 
         transposes(0)
         quantise(0)
@@ -151,14 +145,14 @@ def tile_tiledlinear_kernel(tc, x, weight_words, weight_scales, bias, out):
         sort_words(3)
         for i in (0, 1):
             for c in (0, 1):
-                block(i, c, N_CHUNK)
+                block(i, c)
         transposes(2)
         transposes(3)
         quantise(2)
         quantise(3)
         for c in (2, 3):
             for i in (0, 1):
-                block(i, c, N_CHUNK)
+                block(i, c)
         for i in range(2, ROW_TILES):
             if i % 2 == 1 and i + 2 < ROW_TILES:
                 for j in (i + 1, i + 2):
@@ -167,5 +161,4 @@ def tile_tiledlinear_kernel(tc, x, weight_words, weight_scales, bias, out):
                     transposes(j)
                     quantise(j)
             for c in range(CHUNKS):
-                last = i == ROW_TILES - 1 and c == CHUNKS - 1
-                block(i, c, P if last else N_CHUNK)
+                block(i, c)

@@ -39,7 +39,7 @@ def tile_tiledlinear_kernel(tc, x, weight_words, weight_scales, bias, out):
 
         x_sb = [keep.tile([P, K], BF16, name="x_sb%d" % i) for i in range(ROW_TILES)]
         w_sb = [keep.tile([P, PASSES, 2 * N_CHUNK], U8, name="w_sb%d" % c, align_bytes=64) for c in range(CHUNKS)]
-        w_sc = [keep.tile([P, PASSES, 2 * N_CHUNK], U8, name="w_sc%d" % h, align_bytes=64) for h in range(CHUNKS // 2)]
+        w_sc = [keep.tile([P, PASSES, N_CHUNK], U8, name="w_sc%d" % c, align_bytes=64) for c in range(CHUNKS)]
         x_q = [keep.tile([P, PASSES * P], U32, name="x_q%d" % i, align_bytes=64) for i in range(ROW_TILES)]
         x_qs = [keep.tile([P, PASSES * P], U8, name="x_qs%d" % i, align_bytes=64) for i in range(ROW_TILES)]
         bias_f = [keep.tile([P, N_CHUNK], F32, name="bias_f%d" % c) for c in range(CHUNKS)]
@@ -47,10 +47,10 @@ def tile_tiledlinear_kernel(tc, x, weight_words, weight_scales, bias, out):
         ones = keep.tile([P, P], BF16, name="ones")
         ident = keep.tile([P, P], F32, name="ident")
 
-        nc.vector.memset(w_sc[0][:].bitcast(I32), 0)
         nc.vector.memset(bias_row[:].bitcast(I32), 0)
         nc.vector.memset(ones[:], 1.0)
-        nc.vector.memset(w_sc[1][:].bitcast(I32), 0)
+        for c in range(CHUNKS):
+            nc.vector.memset(w_sc[c][:].bitcast(I32), 0)
         make_identity(nc, ident[:])
 
         def load_x(i, pieces):
@@ -59,10 +59,10 @@ def tile_tiledlinear_kernel(tc, x, weight_words, weight_scales, bias, out):
                 cols = slice(h * width, (h + 1) * width)
                 nc.sync.dma_start(out=x_sb[i][:, cols], in_=x_rows[i * P : (i + 1) * P, cols])
 
-        for h in range(CHUNKS // 2):
-            src = weight_scales[:, :, 2 * h * N_CHUNK : 2 * (h + 1) * N_CHUNK].bitcast(F32).rearrange("g q b -> q g b")
+        def load_scales(c):
+            src = weight_scales[:, :, c * N_CHUNK : (c + 1) * N_CHUNK].bitcast(I32).rearrange("g q b -> q g b")
             for r in range(4):
-                nc.gpsimd.dma_start(out=w_sc[h][r:P:32].bitcast(F32), in_=src[r:16:4])
+                nc.sync.dma_start(out=w_sc[c][r:P:32].bitcast(I32), in_=src[r:16:4])
 
         def load_words(c):
             src = weight_words[:, :, c * 2 * N_CHUNK : (c + 1) * 2 * N_CHUNK].bitcast(I32).rearrange("g p b -> p g b")
@@ -71,11 +71,15 @@ def tile_tiledlinear_kernel(tc, x, weight_words, weight_scales, bias, out):
         load_x(0, 2)
         nc.sync.dma_start(out=bias_row[0:1, :], in_=bias.rearrange("(o n) -> o n", o=1))
         load_x(1, 1)
+        load_scales(0)
         load_words(0)
+        load_scales(1)
         load_words(1)
         load_x(2, 1)
         load_x(3, 1)
+        load_scales(2)
         load_words(2)
+        load_scales(3)
         load_words(3)
         for i in range(4, ROW_TILES):
             load_x(i, 1)
@@ -94,7 +98,7 @@ def tile_tiledlinear_kernel(tc, x, weight_words, weight_scales, bias, out):
             nc.scalar.copy(out=t[:], in_=x_sb[i][:].bitcast(F32).rearrange("r (q u) -> r u q", u=2))
             sorted_words[i] = t
 
-        def transposes(i):
+        def transposes(i, second_copier):
             grp = ring.tile([P, K], BF16, name="grouped", tag="grouped", align_bytes=64)
             grouped[i] = grp
             x32 = x_sb[i][:].bitcast(F32)
@@ -109,7 +113,10 @@ def tile_tiledlinear_kernel(tc, x, weight_words, weight_scales, bias, out):
                             src = x32[:, 256 * g + u : 256 * (g + 1) : 2]
                         nc.tensor.transpose(tp[:, gl, u, :], src, ident[:])
                 dst = grp[:].bitcast(F32)[:, 512 * b : 512 * (b + 1)].rearrange("p (g r u) -> p g r u", g=2, u=2)
-                nc.scalar.copy(out=dst, in_=tp[:].rearrange("p g u r -> p g r u"))
+                if b == 1 and second_copier == "vector":
+                    nc.vector.tensor_copy(out=dst, in_=tp[:].rearrange("p g u r -> p g r u"))
+                else:
+                    nc.scalar.copy(out=dst, in_=tp[:].rearrange("p g u r -> p g r u"))
 
         def quantise(i):
             for b in range(2):
@@ -127,7 +134,7 @@ def tile_tiledlinear_kernel(tc, x, weight_words, weight_scales, bias, out):
                     lhsT=x_q[i][:, g * P : (g + 1) * P].bitcast(FP8X4),
                     lhsT_scale=x_qs[i][:, g * P : (g + 1) * P],
                     rhs=w_sb[c][:, g, :].bitcast(FP4X4),
-                    rhs_scale=w_sc[c // 2][:, g, (c % 2) * N_CHUNK : (c % 2 + 1) * N_CHUNK],
+                    rhs_scale=w_sc[c][:, g, :],
                     start=(g == 0),
                     stop=(g == PASSES - 1),
                 )
@@ -135,19 +142,19 @@ def tile_tiledlinear_kernel(tc, x, weight_words, weight_scales, bias, out):
             nc.vector.tensor_tensor(out=res[:], in0=acc[:], in1=bias_f[c][:], op=ADD)
             nc.sync.dma_start(out=out_rows[i * P : (i + 1) * P, c * N_CHUNK : (c + 1) * N_CHUNK], in_=res[:])
 
-        transposes(0)
+        transposes(0, "vector")
         quantise(0)
         spread_bias()
         sort_words(1)
-        transposes(1)
+        transposes(1, "scalar")
         quantise(1)
         sort_words(2)
         sort_words(3)
         for i in (0, 1):
             for c in (0, 1):
                 block(i, c)
-        transposes(2)
-        transposes(3)
+        transposes(2, "scalar")
+        transposes(3, "scalar")
         quantise(2)
         quantise(3)
         for c in (2, 3):
@@ -158,7 +165,7 @@ def tile_tiledlinear_kernel(tc, x, weight_words, weight_scales, bias, out):
                 for j in (i + 1, i + 2):
                     sort_words(j)
                 for j in (i + 1, i + 2):
-                    transposes(j)
+                    transposes(j, "scalar")
                     quantise(j)
             for c in range(CHUNKS):
                 block(i, c)

@@ -21,6 +21,7 @@ PASSES = K // K_PASS
 N_CHUNK = 512
 CHUNKS = N // N_CHUNK
 ROW_TILES = TOKENS // P
+PE_TILES = 4
 
 FLOPS = 2 * TOKENS * K * N
 
@@ -37,7 +38,8 @@ def tile_tiledlinear_kernel(tc, x, weight_words, weight_scales, bias, out):
         acc_pool = ctx.enter_context(tc.psum_pool(name="acc_pool", bufs=4))
         tp_pool = ctx.enter_context(tc.psum_pool(name="tp_pool", bufs=4))
 
-        x_sb = [keep.tile([P, K], BF16, name="x_sb%d" % i) for i in range(ROW_TILES)]
+        x_sb = [keep.tile([P, K], BF16, name="x_sb%d" % i) for i in range(PE_TILES)]
+        x_quad = {i: keep.tile([P, 16, P], BF16, name="x_quad%d" % i, align_bytes=64) for i in range(PE_TILES, ROW_TILES)}
         w_sb = [keep.tile([P, PASSES, 2 * N_CHUNK], U8, name="w_sb%d" % c, align_bytes=64) for c in range(CHUNKS)]
         w_sc = [keep.tile([P, PASSES, N_CHUNK], U8, name="w_sc%d" % c, align_bytes=64) for c in range(CHUNKS)]
         x_q = [keep.tile([P, PASSES * P], U32, name="x_q%d" % i, align_bytes=64) for i in range(ROW_TILES)]
@@ -58,6 +60,12 @@ def tile_tiledlinear_kernel(tc, x, weight_words, weight_scales, bias, out):
             for h in range(pieces):
                 cols = slice(h * width, (h + 1) * width)
                 nc.sync.dma_start(out=x_sb[i][:, cols], in_=x_rows[i * P : (i + 1) * P, cols])
+
+        def load_quadrants(i):
+            rows = x_rows[i * P : (i + 1) * P, :].rearrange("(r s) k -> r (s k)", s=4)
+            pieces = rows.rearrange("r (m a c) -> a r m c", a=4, c=P)
+            for a in range(4):
+                nc.sync.dma_start(out=x_quad[i][32 * a : 32 * (a + 1), :, :], in_=pieces[a])
 
         def load_scales(c):
             src = weight_scales[:, :, c * N_CHUNK : (c + 1) * N_CHUNK].bitcast(I32).rearrange("g q b -> q g b")
@@ -81,8 +89,8 @@ def tile_tiledlinear_kernel(tc, x, weight_words, weight_scales, bias, out):
         load_words(2)
         load_scales(3)
         load_words(3)
-        for i in range(4, ROW_TILES):
-            load_x(i, 1)
+        for i in range(PE_TILES, ROW_TILES):
+            load_quadrants(i)
 
         def spread_bias():
             for c in range(CHUNKS):
@@ -117,6 +125,28 @@ def tile_tiledlinear_kernel(tc, x, weight_words, weight_scales, bias, out):
                     nc.vector.tensor_copy(out=dst, in_=tp[:].rearrange("p g u r -> p g r u"))
                 else:
                     nc.scalar.copy(out=dst, in_=tp[:].rearrange("p g u r -> p g r u"))
+
+        v_in = {}
+        v_out = {}
+
+        def sort_quadrants(i):
+            t = ring.tile([P, 4, 2, P], F32, name="v_in", tag="v_in", align_bytes=64)
+            words = x_quad[i][:].rearrange("p m c -> p (m c)").bitcast(F32)
+            nc.scalar.copy(out=t[:], in_=words.rearrange("p (s q u) -> p s u q", s=4, u=2))
+            v_in[i] = t
+
+        def vector_transposes(i):
+            t = ring.tile([P, K // 2], F32, name="v_out", tag="v_out", align_bytes=64)
+            nc.vector.transpose(out=t[:], in_=v_in[i][:].rearrange("p s u q -> p (s u q)"))
+            v_out[i] = t
+
+        def weave(i):
+            grp = ring.tile([P, K], BF16, name="grouped", tag="grouped", align_bytes=64)
+            grouped[i] = grp
+            nc.scalar.copy(
+                out=grp[:].bitcast(F32).rearrange("p (q a) -> p q a", a=8),
+                in_=v_out[i][:].rearrange("p (a q) -> p q a", a=8),
+            )
 
         def quantise(i):
             for b in range(2):
@@ -160,12 +190,16 @@ def tile_tiledlinear_kernel(tc, x, weight_words, weight_scales, bias, out):
         for c in (2, 3):
             for i in (0, 1):
                 block(i, c)
+        sort_quadrants(PE_TILES)
         for i in range(2, ROW_TILES):
-            if i % 2 == 1 and i + 2 < ROW_TILES:
-                for j in (i + 1, i + 2):
-                    sort_words(j)
-                for j in (i + 1, i + 2):
-                    transposes(j, "scalar")
-                    quantise(j)
-            for c in range(CHUNKS):
-                block(i, c)
+            block(i, 0)
+            if PE_TILES <= i + 1 < ROW_TILES:
+                quantise(i + 1)
+            block(i, 1)
+            if PE_TILES <= i + 2 < ROW_TILES:
+                vector_transposes(i + 2)
+                weave(i + 2)
+            if PE_TILES <= i + 3 < ROW_TILES:
+                sort_quadrants(i + 3)
+            block(i, 2)
+            block(i, 3)

@@ -21,7 +21,7 @@ PASSES = K // K_PASS
 N_CHUNK = 512
 CHUNKS = N // N_CHUNK
 ROW_TILES = TOKENS // P
-PE_TILES = 4
+PE_TILES = 6
 
 FLOPS = 2 * TOKENS * K * N
 
@@ -89,6 +89,8 @@ def tile_tiledlinear_kernel(tc, x, weight_words, weight_scales, bias, out):
         load_words(2)
         load_scales(3)
         load_words(3)
+        for i in range(4, PE_TILES):
+            load_x(i, 1)
         for i in range(PE_TILES, ROW_TILES):
             load_quadrants(i)
 
@@ -190,16 +192,21 @@ def tile_tiledlinear_kernel(tc, x, weight_words, weight_scales, bias, out):
         for c in (2, 3):
             for i in (0, 1):
                 block(i, c)
-        sort_quadrants(PE_TILES)
         for i in range(2, ROW_TILES):
+            if i % 2 == 1 and i + 2 < PE_TILES:
+                for j in (i + 1, i + 2):
+                    sort_words(j)
+                for j in (i + 1, i + 2):
+                    transposes(j, "scalar")
+                    quantise(j)
+            if i == 3:
+                sort_quadrants(6)
+                sort_quadrants(7)
             block(i, 0)
-            if PE_TILES <= i + 1 < ROW_TILES:
-                quantise(i + 1)
-            block(i, 1)
-            if PE_TILES <= i + 2 < ROW_TILES:
-                vector_transposes(i + 2)
-                weave(i + 2)
-            if PE_TILES <= i + 3 < ROW_TILES:
-                sort_quadrants(i + 3)
-            block(i, 2)
-            block(i, 3)
+            if i in (3, 5):
+                vector_transposes((i + 9) // 2)
+                weave((i + 9) // 2)
+            if i in (4, 6):
+                quantise((i + 8) // 2)
+            for c in range(1, CHUNKS):
+                block(i, c)

@@ -21,7 +21,7 @@ PASSES = K // K_PASS
 N_CHUNK = 512
 CHUNKS = N // N_CHUNK
 ROW_TILES = TOKENS // P
-PE_TILES = 6
+PE_TILES = 5
 
 FLOPS = 2 * TOKENS * K * N
 
@@ -192,21 +192,24 @@ def tile_tiledlinear_kernel(tc, x, weight_words, weight_scales, bias, out):
         for c in (2, 3):
             for i in (0, 1):
                 block(i, c)
+        sort_quadrants(5)
         for i in range(2, ROW_TILES):
-            if i % 2 == 1 and i + 2 < PE_TILES:
-                for j in (i + 1, i + 2):
-                    sort_words(j)
-                for j in (i + 1, i + 2):
-                    transposes(j, "scalar")
-                    quantise(j)
             if i == 3:
+                sort_words(4)
+                transposes(4, "scalar")
+                quantise(4)
                 sort_quadrants(6)
-                sort_quadrants(7)
             block(i, 0)
-            if i in (3, 5):
-                vector_transposes((i + 9) // 2)
-                weave((i + 9) // 2)
-            if i in (4, 6):
-                quantise((i + 8) // 2)
-            for c in range(1, CHUNKS):
-                block(i, c)
+            if i in (3, 4, 6):
+                quantise({3: 5, 4: 6, 6: 7}[i])
+            if i == 5:
+                vector_transposes(7)
+                weave(7)
+            block(i, 1)
+            block(i, 2)
+            if i in (2, 3):
+                vector_transposes(i + 3)
+                weave(i + 3)
+            if i == 3:
+                sort_quadrants(7)
+            block(i, 3)

@@ -192,24 +192,19 @@ def tile_tiledlinear_kernel(tc, x, weight_words, weight_scales, bias, out):
         for c in (2, 3):
             for i in (0, 1):
                 block(i, c)
-        sort_quadrants(5)
+        sort_words(4)
         for i in range(2, ROW_TILES):
-            if i == 3:
-                sort_words(4)
-                transposes(4, "scalar")
-                quantise(4)
-                sort_quadrants(6)
             block(i, 0)
-            if i in (3, 4, 6):
-                quantise({3: 5, 4: 6, 6: 7}[i])
-            if i == 5:
-                vector_transposes(7)
-                weave(7)
             block(i, 1)
+            if i == 2:
+                transposes(4, "scalar")
+                sort_quadrants(5)
             block(i, 2)
-            if i in (2, 3):
+            if i + 2 < ROW_TILES:
+                quantise(i + 2)
+            block(i, 3)
+            if PE_TILES <= i + 3 < ROW_TILES:
                 vector_transposes(i + 3)
                 weave(i + 3)
-            if i == 3:
-                sort_quadrants(7)
-            block(i, 3)
+            if PE_TILES <= i + 4 < ROW_TILES:
+                sort_quadrants(i + 4)

@@ -145,10 +145,10 @@ def tile_tiledlinear_kernel(tc, x, weight_words, weight_scales, bias, out):
         def weave(i):
             grp = ring.tile([P, K], BF16, name="grouped", tag="grouped", align_bytes=64)
             grouped[i] = grp
-            nc.scalar.copy(
-                out=grp[:].bitcast(F32).rearrange("p (q a) -> p q a", a=8),
-                in_=v_out[i][:].rearrange("p (a q) -> p q a", a=8),
-            )
+            dst = grp[:].bitcast(F32).rearrange("p (q a) -> p q a", a=8)
+            src = v_out[i][:].rearrange("p (a q) -> p q a", a=8)
+            for h in range(2):
+                nc.scalar.copy(out=dst[:, :, 4 * h : 4 * (h + 1)], in_=src[:, :, 4 * h : 4 * (h + 1)])
 
         def quantise(i):
             for b in range(2):
@@ -171,7 +171,12 @@ def tile_tiledlinear_kernel(tc, x, weight_words, weight_scales, bias, out):
                     stop=(g == PASSES - 1),
                 )
             res = keep.tile([P, N_CHUNK], F32, name="res%d_%d" % (i, c))
-            nc.vector.tensor_tensor(out=res[:], in0=acc[:], in1=bias_f[c][:], op=ADD)
+            if c == 0 and 2 <= i < ROW_TILES - 1:
+                raw = ring.tile([P, N_CHUNK], F32, name="raw", tag="raw")
+                nc.scalar.copy(out=raw[:], in_=acc[:])
+                nc.gpsimd.tensor_tensor(out=res[:], in0=raw[:], in1=bias_f[c][:], op=ADD)
+            else:
+                nc.vector.tensor_tensor(out=res[:], in0=acc[:], in1=bias_f[c][:], op=ADD)
             nc.sync.dma_start(out=out_rows[i * P : (i + 1) * P, c * N_CHUNK : (c + 1) * N_CHUNK], in_=res[:])
 
         transposes(0, "vector")
@@ -195,6 +200,10 @@ def tile_tiledlinear_kernel(tc, x, weight_words, weight_scales, bias, out):
         sort_words(4)
         for i in range(2, ROW_TILES):
             block(i, 0)
+            if PE_TILES <= i + 2 < ROW_TILES:
+                weave(i + 2)
+            if PE_TILES <= i + 3 < ROW_TILES and i > 2:
+                sort_quadrants(i + 3)
             block(i, 1)
             if i == 2:
                 transposes(4, "scalar")
@@ -205,6 +214,3 @@ def tile_tiledlinear_kernel(tc, x, weight_words, weight_scales, bias, out):
             block(i, 3)
             if PE_TILES <= i + 3 < ROW_TILES:
                 vector_transposes(i + 3)
-                weave(i + 3)
-            if PE_TILES <= i + 4 < ROW_TILES:
-                sort_quadrants(i + 4)

@@ -98,14 +98,21 @@ def tile_tiledlinear_kernel(tc, x, weight_words, weight_scales, bias, out):
             for c in range(CHUNKS):
                 acc = acc_pool.tile([P, N_CHUNK], F32, name="acc", tag="acc")
                 nc.tensor.matmul(out=acc[:], lhsT=ones[:], rhs=bias_row[:, c * N_CHUNK : (c + 1) * N_CHUNK], start=True, stop=True)
-                nc.vector.tensor_copy(out=bias_f[c][:], in_=acc[:])
+                if c < 2:
+                    nc.scalar.copy(out=bias_f[c][:], in_=acc[:])
+                else:
+                    nc.vector.tensor_copy(out=bias_f[c][:], in_=acc[:])
 
         sorted_words = {}
         grouped = {}
 
-        def sort_words(i):
+        def sort_words(i, engine):
             t = ring.tile([P, 2, K // 4], F32, name="sorted_w", tag="sorted_w")
-            nc.scalar.copy(out=t[:], in_=x_sb[i][:].bitcast(F32).rearrange("r (q u) -> r u q", u=2))
+            words = x_sb[i][:].bitcast(F32).rearrange("r (q u) -> r u q", u=2)
+            if engine == "vector":
+                nc.vector.tensor_copy(out=t[:], in_=words)
+            else:
+                nc.scalar.copy(out=t[:], in_=words)
             sorted_words[i] = t
 
         def transposes(i, second_copier):
@@ -182,14 +189,14 @@ def tile_tiledlinear_kernel(tc, x, weight_words, weight_scales, bias, out):
         transposes(0, "vector")
         quantise(0)
         spread_bias()
-        sort_words(1)
         transposes(1, "scalar")
         quantise(1)
-        sort_words(2)
-        sort_words(3)
-        for i in (0, 1):
-            for c in (0, 1):
-                block(i, c)
+        sort_words(2, "scalar")
+        block(0, 0)
+        block(1, 0)
+        block(0, 1)
+        sort_words(3, "vector")
+        block(1, 1)
         transposes(2, "scalar")
         transposes(3, "scalar")
         quantise(2)
@@ -197,7 +204,7 @@ def tile_tiledlinear_kernel(tc, x, weight_words, weight_scales, bias, out):
         for c in (2, 3):
             for i in (0, 1):
                 block(i, c)
-        sort_words(4)
+        sort_words(4, "scalar")
         for i in range(2, ROW_TILES):
             block(i, 0)
             if PE_TILES <= i + 2 < ROW_TILES:

from contextlib import ExitStack

import concourse.mybir as mybir
from concourse.masks import make_identity

F32 = mybir.dt.float32
BF16 = mybir.dt.bfloat16
I32 = mybir.dt.int32
U32 = mybir.dt.uint32
U8 = mybir.dt.uint8
FP8X4 = mybir.dt.float8_e4m3fn_x4
FP4X4 = mybir.dt.float4_e2m1fn_x4
ADD = mybir.AluOpType.add

P = 128
TOKENS = 1024
K = 2048
N = 2048
K_PASS = 512
PASSES = K // K_PASS
N_CHUNK = 512
CHUNKS = N // N_CHUNK
ROW_TILES = TOKENS // P
PE_TILES = 5

FLOPS = 2 * TOKENS * K * N


def tile_tiledlinear_kernel(tc, x, weight_words, weight_scales, bias, out):
    nc = tc.nc
    x_rows = x.flatten_outer_dims()
    out_rows = out.flatten_outer_dims()

    with ExitStack() as ctx:
        ctx.enter_context(tc.manual_schedule())
        keep = ctx.enter_context(tc.tile_pool(name="keep", bufs=1))
        ring = ctx.enter_context(tc.tile_pool(name="ring", bufs=4))
        acc_pool = ctx.enter_context(tc.psum_pool(name="acc_pool", bufs=4))
        tp_pool = ctx.enter_context(tc.psum_pool(name="tp_pool", bufs=4))

        x_sb = [keep.tile([P, K], BF16, name="x_sb%d" % i) for i in range(PE_TILES)]
        x_quad = {i: keep.tile([P, 16, P], BF16, name="x_quad%d" % i, align_bytes=64) for i in range(PE_TILES, ROW_TILES)}
        w_sb = [keep.tile([P, PASSES, 2 * N_CHUNK], U8, name="w_sb%d" % c, align_bytes=64) for c in range(CHUNKS)]
        w_sc = [keep.tile([P, PASSES, N_CHUNK], U8, name="w_sc%d" % c, align_bytes=64) for c in range(CHUNKS)]
        x_q = [keep.tile([P, PASSES * P], U32, name="x_q%d" % i, align_bytes=64) for i in range(ROW_TILES)]
        x_qs = [keep.tile([P, PASSES * P], U8, name="x_qs%d" % i, align_bytes=64) for i in range(ROW_TILES)]
        bias_f = [keep.tile([P, N_CHUNK], F32, name="bias_f%d" % c) for c in range(CHUNKS)]
        bias_row = keep.tile([P, N], BF16, name="bias_row")
        ones = keep.tile([P, P], BF16, name="ones")
        ident = keep.tile([P, P], F32, name="ident")

        nc.vector.memset(bias_row[:].bitcast(I32), 0)
        nc.vector.memset(ones[:], 1.0)
        for c in range(CHUNKS):
            nc.vector.memset(w_sc[c][:].bitcast(I32), 0)
        make_identity(nc, ident[:])

        def load_x(i, pieces):
            width = K // pieces
            for h in range(pieces):
                cols = slice(h * width, (h + 1) * width)
                nc.sync.dma_start(out=x_sb[i][:, cols], in_=x_rows[i * P : (i + 1) * P, cols])

        def load_quadrants(i):
            rows = x_rows[i * P : (i + 1) * P, :].rearrange("(r s) k -> r (s k)", s=4)
            pieces = rows.rearrange("r (m a c) -> a r m c", a=4, c=P)
            for a in range(4):
                nc.sync.dma_start(out=x_quad[i][32 * a : 32 * (a + 1), :, :], in_=pieces[a])

        def load_scales(c):
            src = weight_scales[:, :, c * N_CHUNK : (c + 1) * N_CHUNK].bitcast(I32).rearrange("g q b -> q g b")
            for r in range(4):
                nc.sync.dma_start(out=w_sc[c][r:P:32].bitcast(I32), in_=src[r:16:4])

        def load_words(c):
            src = weight_words[:, :, c * 2 * N_CHUNK : (c + 1) * 2 * N_CHUNK].bitcast(I32).rearrange("g p b -> p g b")
            nc.sync.dma_start(out=w_sb[c][:].bitcast(I32), in_=src)

        load_x(0, 2)
        nc.sync.dma_start(out=bias_row[0:1, :], in_=bias.rearrange("(o n) -> o n", o=1))
        load_x(1, 1)
        load_scales(0)
        load_words(0)
        load_scales(1)
        load_words(1)
        load_x(2, 1)
        load_x(3, 1)
        load_scales(2)
        load_words(2)
        load_scales(3)
        load_words(3)
        for i in range(4, PE_TILES):
            load_x(i, 1)
        for i in range(PE_TILES, ROW_TILES):
            load_quadrants(i)

        def spread_bias():
            for c in range(CHUNKS):
                acc = acc_pool.tile([P, N_CHUNK], F32, name="acc", tag="acc")
                nc.tensor.matmul(out=acc[:], lhsT=ones[:], rhs=bias_row[:, c * N_CHUNK : (c + 1) * N_CHUNK], start=True, stop=True)
                if c < 2:
                    nc.scalar.copy(out=bias_f[c][:], in_=acc[:])
                else:
                    nc.vector.tensor_copy(out=bias_f[c][:], in_=acc[:])

        sorted_words = {}
        grouped = {}

        def sort_words(i, engine):
            t = ring.tile([P, 2, K // 4], F32, name="sorted_w", tag="sorted_w")
            words = x_sb[i][:].bitcast(F32).rearrange("r (q u) -> r u q", u=2)
            if engine == "vector":
                nc.vector.tensor_copy(out=t[:], in_=words)
            else:
                nc.scalar.copy(out=t[:], in_=words)
            sorted_words[i] = t

        def transposes(i, second_copier):
            grp = ring.tile([P, K], BF16, name="grouped", tag="grouped", align_bytes=64)
            grouped[i] = grp
            x32 = x_sb[i][:].bitcast(F32)
            for b in range(2):
                tp = tp_pool.tile([P, 2, 2, P], F32, name="tp", tag="tp")
                for gl in range(2):
                    g = 2 * b + gl
                    for u in range(2):
                        if i in sorted_words:
                            src = sorted_words[i][:, u, g * P : (g + 1) * P]
                        else:
                            src = x32[:, 256 * g + u : 256 * (g + 1) : 2]
                        nc.tensor.transpose(tp[:, gl, u, :], src, ident[:])
                dst = grp[:].bitcast(F32)[:, 512 * b : 512 * (b + 1)].rearrange("p (g r u) -> p g r u", g=2, u=2)
                if b == 1 and second_copier == "vector":
                    nc.vector.tensor_copy(out=dst, in_=tp[:].rearrange("p g u r -> p g r u"))
                else:
                    nc.scalar.copy(out=dst, in_=tp[:].rearrange("p g u r -> p g r u"))

        v_in = {}
        v_out = {}

        def sort_quadrants(i):
            t = ring.tile([P, 4, 2, P], F32, name="v_in", tag="v_in", align_bytes=64)
            words = x_quad[i][:].rearrange("p m c -> p (m c)").bitcast(F32)
            nc.scalar.copy(out=t[:], in_=words.rearrange("p (s q u) -> p s u q", s=4, u=2))
            v_in[i] = t

        def vector_transposes(i):
            t = ring.tile([P, K // 2], F32, name="v_out", tag="v_out", align_bytes=64)
            nc.vector.transpose(out=t[:], in_=v_in[i][:].rearrange("p s u q -> p (s u q)"))
            v_out[i] = t

        def weave(i):
            grp = ring.tile([P, K], BF16, name="grouped", tag="grouped", align_bytes=64)
            grouped[i] = grp
            dst = grp[:].bitcast(F32).rearrange("p (q a) -> p q a", a=8)
            src = v_out[i][:].rearrange("p (a q) -> p q a", a=8)
            for h in range(2):
                nc.scalar.copy(out=dst[:, :, 4 * h : 4 * (h + 1)], in_=src[:, :, 4 * h : 4 * (h + 1)])

        def quantise(i):
            for b in range(2):
                nc.vector.quantize_mx(
                    out=x_q[i][:, 256 * b : 256 * (b + 1)].bitcast(FP8X4),
                    scales=x_qs[i][:, 256 * b : 256 * (b + 1)],
                    in_=grouped[i][:, 1024 * b : 1024 * (b + 1)],
                )

        def block(i, c):
            acc = acc_pool.tile([P, N_CHUNK], F32, name="acc", tag="acc")
            for g in range(PASSES):
                nc.tensor.matmul_mx(
                    out=acc[:],
                    lhsT=x_q[i][:, g * P : (g + 1) * P].bitcast(FP8X4),
                    lhsT_scale=x_qs[i][:, g * P : (g + 1) * P],
                    rhs=w_sb[c][:, g, :].bitcast(FP4X4),
                    rhs_scale=w_sc[c][:, g, :],
                    start=(g == 0),
                    stop=(g == PASSES - 1),
                )
            res = keep.tile([P, N_CHUNK], F32, name="res%d_%d" % (i, c))
            if c == 0 and 2 <= i < ROW_TILES - 1:
                raw = ring.tile([P, N_CHUNK], F32, name="raw", tag="raw")
                nc.scalar.copy(out=raw[:], in_=acc[:])
                nc.gpsimd.tensor_tensor(out=res[:], in0=raw[:], in1=bias_f[c][:], op=ADD)
            else:
                nc.vector.tensor_tensor(out=res[:], in0=acc[:], in1=bias_f[c][:], op=ADD)
            nc.sync.dma_start(out=out_rows[i * P : (i + 1) * P, c * N_CHUNK : (c + 1) * N_CHUNK], in_=res[:])

        transposes(0, "vector")
        quantise(0)
        spread_bias()
        transposes(1, "scalar")
        quantise(1)
        sort_words(2, "scalar")
        block(0, 0)
        block(1, 0)
        block(0, 1)
        sort_words(3, "vector")
        block(1, 1)
        transposes(2, "scalar")
        transposes(3, "scalar")
        quantise(2)
        quantise(3)
        for c in (2, 3):
            for i in (0, 1):
                block(i, c)
        sort_words(4, "scalar")
        for i in range(2, ROW_TILES):
            block(i, 0)
            if PE_TILES <= i + 2 < ROW_TILES:
                weave(i + 2)
            if PE_TILES <= i + 3 < ROW_TILES and i > 2:
                sort_quadrants(i + 3)
            block(i, 1)
            if i == 2:
                transposes(4, "scalar")
                sort_quadrants(5)
            block(i, 2)
            if i + 2 < ROW_TILES:
                quantise(i + 2)
            block(i, 3)
            if PE_TILES <= i + 3 < ROW_TILES:
                vector_transposes(i + 3)
